import numpy as np
import ml_dtypes


def mxq(x, axis, fmt="e4m3"):
    dtype, down = {"e4m3": (ml_dtypes.float8_e4m3fn, 7), "e5m2": (ml_dtypes.float8_e5m2, 14)}[fmt]
    v = np.moveaxis(np.asarray(x, np.float32).astype(ml_dtypes.bfloat16).astype(np.float64), axis, -1)
    blocks = v.reshape(v.shape[:-1] + (-1, 32))
    amax = np.abs(blocks).max(-1, keepdims=True)
    byte = np.maximum(np.where(amax > 0, np.frexp(amax)[1] - 1 + 127, 0) - down, 1)
    scale = np.exp2(byte - 127.0)
    codes = (blocks / scale).astype(np.float32).astype(dtype).astype(np.float64)
    return np.moveaxis((codes * scale).reshape(v.shape), -1, axis)


WIDE = False


def mx_kscale(k):
    if not WIDE:
        return np.ones(k)
    levels = np.array([10, -10, 5, -5, 0])
    if k % 512:
        return np.exp2(np.random.permutation(np.resize(levels, k // 32))).repeat(32)
    a = np.empty((k // 512, 16))
    for p in range(k // 512):
        a[p, :8] = np.random.permutation(np.resize(levels, 8))
        for g in range(8):
            far = levels[np.abs(levels - a[p, g]) >= 10]
            a[p, g + 8] = far[np.random.randint(len(far))]
    return np.exp2(a.ravel()).repeat(32)


BF16 = ml_dtypes.bfloat16


def bf(x):
    return np.asarray(x, np.float32).astype(BF16)


def f64(x):
    return np.asarray(x).astype(np.float64)


NB, S, D, O, E, R = 4, 1024, 1024, 256, 32, 16
ER = E * R
SCALING = 2.0


def softmax(v):
    e = np.exp(v - v.max(-1, keepdims=True))
    return e / e.sum(-1, keepdims=True)


def setup_inputs():
    s, t = mx_kscale(D), mx_kscale(ER)
    return {
        "x": bf(np.random.standard_normal((NB, S, D)) * s),
        "gate_logits": bf(np.random.standard_normal((NB, S, E)) * 1.5),
        "W_base": bf(np.random.standard_normal((O, D)) / np.sqrt(D) / s),
        "b_base": bf(np.random.standard_normal(O) * 0.3),
        "A": bf(np.random.standard_normal((E, R, D)) / np.sqrt(D) / s * t.reshape(E, R, 1)),
        "B": bf(np.random.standard_normal((E, O, R)) / np.sqrt(R) / t.reshape(E, 1, R)),
    }


def reference(x, gate_logits, W_base, b_base, A, B):
    xq = mxq(f64(x), 2, "e4m3")
    result = (xq @ mxq(f64(W_base), 1, "e4m3").T) + f64(b_base)
    route = softmax(f64(gate_logits))
    h = (xq @ mxq(f64(A).reshape(ER, D), 1, "e4m3").T).reshape(NB, S, E, R)
    hw = (h * route[..., None]).reshape(NB, S, ER)
    b_flat = f64(B).transpose(0, 2, 1).reshape(ER, O)
    return result + SCALING * (mxq(hw, 2, "e4m3") @ mxq(b_flat, 0, "e4m3"))

@@ -1,0 +1,351 @@
+from contextlib import ExitStack
+
+import concourse.masks as masks
+import concourse.mybir as mybir
+
+F32 = mybir.dt.float32
+BF16 = mybir.dt.bfloat16
+U32 = mybir.dt.uint32
+U8 = mybir.dt.uint8
+FP8X4 = mybir.dt.float8_e4m3fn_x4
+ALU = mybir.AluOpType
+ACT = mybir.ActivationFunctionType
+AXIS = mybir.AxisListType
+
+P = 128
+PACK = 4
+TOKENS = 4096
+D = 1024
+O = 256
+E = 32
+RANK = 16
+ER = E * RANK
+SCALING = 2.0
+PASSES = D // (P * PACK)
+WORDS = D // 2
+BANK = 512
+SLOTS = TOKENS // P
+UNIT = 2
+UNITS = SLOTS // UNIT
+O_TILES = O // P
+LAG = 4
+
+FLOPS = 2 * TOKENS * D * (O + ER) + 2 * TOKENS * ER * O
+
+
+def tile_linearmoloralayer_pa_t_kernel(tc, x, gate_logits, W_base, b_base, A, B, out):
+    nc = tc.nc
+
+    x_view = x.flatten_outer_dims().rearrange("(p s) d -> p s d", s=SLOTS)
+    gate_view = gate_logits.flatten_outer_dims().rearrange("(p s) e -> p (s e)", s=SLOTS)
+    out_view = out.flatten_outer_dims().rearrange("(p s) o -> p s o", s=SLOTS)
+    a_view = A.flatten_outer_dims().rearrange("(q c) d -> q c d", c=PACK)
+    w_view = W_base.rearrange("(h m) d -> m h d", m=P)
+    b_view = B.rearrange("e (m h) r -> m e (h r)", h=O_TILES)
+
+    with ExitStack() as ctx:
+        keep = ctx.enter_context(tc.tile_pool(name="keep", bufs=1))
+        xg_pool = ctx.enter_context(tc.tile_pool(name="xg_pool", bufs=2))
+        xq_pool = ctx.enter_context(tc.tile_pool(name="xq_pool", bufs=LAG + 2))
+        route_pool = ctx.enter_context(tc.tile_pool(name="route_pool", bufs=2))
+        hwg_pool = ctx.enter_context(tc.tile_pool(name="hwg_pool", bufs=2))
+        hwq_pool = ctx.enter_context(tc.tile_pool(name="hwq_pool", bufs=LAG + 1))
+        stage_pool = ctx.enter_context(tc.tile_pool(name="stage_pool", bufs=6))
+        t_psum = ctx.enter_context(tc.psum_pool(name="t_psum", bufs=4))
+        h_psum = ctx.enter_context(tc.psum_pool(name="h_psum", bufs=2))
+        o_psum = ctx.enter_context(tc.psum_pool(name="o_psum", bufs=2))
+        ctx.enter_context(tc.manual_schedule())
+
+        ident = keep.tile([P, P], F32)
+        masks.make_identity(nc, ident[:])
+
+        gate_sb = keep.tile([P, SLOTS * E], BF16)
+        a_raw = [keep.tile([P, D], BF16, name="a_raw%d" % c) for c in range(PACK)]
+        x_raw = [keep.tile([P, D], BF16, name="x_raw%d" % s) for s in range(SLOTS)]
+        w_raw = keep.tile([P, O_TILES * D], BF16)
+        b_raw = keep.tile([P, O_TILES * ER], BF16)
+        bias_sb = keep.tile([P, O], BF16)
+
+        def load_x(first, last):
+            for s in range(first, last):
+                nc.sync.dma_start(out=x_raw[s][:], in_=x_view[:, s, :])
+
+        nc.sync.dma_start(out=gate_sb[:], in_=gate_view)
+        for c in range(PACK):
+            nc.sync.dma_start(out=a_raw[c][:], in_=a_view[:, c, :])
+        load_x(0, LAG * UNIT)
+        nc.sync.dma_start(out=w_raw[:].rearrange("m (h d) -> m h d", h=O_TILES), in_=w_view)
+        nc.sync.dma_start(out=b_raw[:].rearrange("m (e f) -> m e f", e=E), in_=b_view)
+        load_x(LAG * UNIT, 2 * LAG * UNIT)
+        nc.sync.dma_start(out=bias_sb[:], in_=b_base.partition_broadcast(P))
+        load_x(2 * LAG * UNIT, SLOTS)
+
+        def transpose_rows(bank, words):
+            for g in range(PASSES):
+                for u in range(2):
+                    cols = slice((g * 2 + u) * P, (g * 2 + u + 1) * P)
+                    every_second = slice(g * 2 * P + u, (g + 1) * 2 * P, 2)
+                    nc.tensor.transpose(out=bank[:, cols], in_=words[:, every_second], identity=ident[:])
+
+        def words_side_by_side(bank):
+            return bank[:].rearrange("q (g u m) -> q g m u", g=PASSES, u=2)
+
+        g_max = keep.tile([P, SLOTS], F32)
+        g_exp = keep.tile([P, SLOTS * E], F32)
+        g_sum = keep.tile([P, SLOTS], F32)
+        g_inv = keep.tile([P, SLOTS], F32)
+        route_wide = {}
+        route_t = {}
+
+        def by_slot(ap):
+            return ap.rearrange("p (s e) -> p s e", e=E)
+
+        def softmax_shift(first, last):
+            cols = slice(first * E, last * E)
+            nc.vector.tensor_reduce(
+                out=g_max[:, first:last], in_=by_slot(gate_sb[:, cols]), axis=AXIS.X, op=ALU.max
+            )
+            nc.vector.tensor_tensor(
+                out=by_slot(g_exp[:, cols]),
+                in0=by_slot(gate_sb[:, cols]),
+                in1=g_max[:, first:last].unsqueeze(2).to_broadcast([P, last - first, E]),
+                op=ALU.subtract,
+            )
+
+        def softmax_exp_norm(first, last):
+            cols = slice(first * E, last * E)
+            nc.scalar.activation(out=g_exp[:, cols], in_=g_exp[:, cols], func=ACT.Exp)
+            nc.vector.tensor_reduce(
+                out=g_sum[:, first:last], in_=by_slot(g_exp[:, cols]), axis=AXIS.X, op=ALU.add
+            )
+            nc.vector.reciprocal(out=g_inv[:, first:last], in_=g_sum[:, first:last])
+
+        def expand_route(n):
+            first = n * UNIT
+            wide = route_pool.tile([P, UNIT * P], F32, name="route_wide", tag="route_wide")
+            route_wide[n] = wide
+            shape = [P, UNIT, E, PACK]
+            nc.gpsimd.tensor_tensor(
+                out=wide[:].rearrange("p (j e i) -> p j e i", j=UNIT, i=PACK),
+                in0=by_slot(g_exp[:, first * E : (first + UNIT) * E]).unsqueeze(3).to_broadcast(shape),
+                in1=g_inv[:, first : first + UNIT].unsqueeze(2).unsqueeze(3).to_broadcast(shape),
+                op=ALU.mult,
+            )
+
+        def transpose_route(n):
+            bank = t_psum.tile([P, UNIT * P], F32, name="route_bank", tag="t")
+            for j in range(UNIT):
+                cols = slice(j * P, (j + 1) * P)
+                nc.tensor.transpose(out=bank[:, cols], in_=route_wide[n][:, cols], identity=ident[:])
+            route_t[n] = route_pool.tile([P, UNIT * P], F32, name="route_t", tag="route_t")
+            nc.scalar.mul(out=route_t[n][:], in_=bank[:], mul=SCALING)
+
+        a_grouped = keep.tile([P, PACK * D], BF16, align_bytes=64)
+        a_codes = keep.tile([P, PACK * PASSES * P], U32, align_bytes=64)
+        a_scales = keep.tile([P, PACK * PASSES * P], U8, align_bytes=64)
+        w_grouped = keep.tile([P, O_TILES * D], BF16, align_bytes=64)
+        w_codes = keep.tile([P, PASSES * O], U32, align_bytes=64)
+        w_scales = keep.tile([P, PASSES * O], U8, align_bytes=64)
+        b_sorted = keep.tile([P, O_TILES * ER], BF16)
+        b_grouped = keep.tile([P, O * PACK], BF16, align_bytes=64)
+        b_codes = keep.tile([P, O], U32, align_bytes=64)
+        b_scales = keep.tile([P, O], U8, align_bytes=64)
+
+        def prepare_a_chunk(c):
+            bank = t_psum.tile([P, BANK], F32, name="a_bank", tag="t")
+            transpose_rows(bank, a_raw[c][:].bitcast(F32))
+            grouped_words = a_grouped[:].bitcast(F32).rearrange(
+                "q (c g m u) -> q c g m u", c=PACK, g=PASSES, u=2
+            )
+            nc.scalar.copy(out=grouped_words[:, c], in_=words_side_by_side(bank))
+            cols = slice(c * PASSES * P, (c + 1) * PASSES * P)
+            nc.vector.quantize_mx(
+                out=a_codes[:, cols].bitcast(FP8X4),
+                scales=a_scales[:, cols],
+                in_=a_grouped[:, c * D : (c + 1) * D],
+            )
+
+        def transpose_w():
+            grouped_words = w_grouped[:].bitcast(F32).rearrange(
+                "q (g h m u) -> q g h m u", g=PASSES, h=O_TILES, u=2
+            )
+            for h in range(O_TILES):
+                bank = t_psum.tile([P, BANK], F32, name="w_bank", tag="t")
+                transpose_rows(bank, w_raw[:].bitcast(F32)[:, h * WORDS : (h + 1) * WORDS])
+                nc.scalar.copy(out=grouped_words[:, :, h], in_=words_side_by_side(bank))
+
+        def quantise_w():
+            nc.vector.quantize_mx(
+                out=w_codes[:].bitcast(FP8X4), scales=w_scales[:], in_=w_grouped[:]
+            )
+
+        def sort_b():
+            nc.vector.tensor_copy(
+                out=b_sorted[:].rearrange("m (h e r) -> m h e r", h=O_TILES, r=RANK),
+                in_=b_raw[:].rearrange("m (e h r) -> m h e r", h=O_TILES, r=RANK),
+            )
+
+        def transpose_b():
+            words = b_sorted[:].bitcast(F32).rearrange("m (h q u) -> m h u q", h=O_TILES, u=2)
+            bank = t_psum.tile([P, BANK], F32, name="b_bank", tag="t")
+            for h in range(O_TILES):
+                for u in range(2):
+                    cols = slice((h * 2 + u) * P, (h * 2 + u + 1) * P)
+                    nc.tensor.transpose(out=bank[:, cols], in_=words[:, h, u, :], identity=ident[:])
+            nc.scalar.copy(
+                out=b_grouped[:].bitcast(F32).rearrange("q (m h u) -> q m h u", h=O_TILES, u=2),
+                in_=bank[:].rearrange("q (h u m) -> q m h u", h=O_TILES, u=2),
+            )
+
+        def quantise_b():
+            nc.vector.quantize_mx(
+                out=b_codes[:].bitcast(FP8X4), scales=b_scales[:], in_=b_grouped[:]
+            )
+
+        x_grouped = {}
+        x_codes = {}
+        x_scales = {}
+
+        def transpose_x(n):
+            x_grouped[n] = xg_pool.tile([P, UNIT * D], BF16, name="x_grouped", tag="xg", align_bytes=64)
+            grouped_words = x_grouped[n][:].bitcast(F32).rearrange(
+                "q (j g w u) -> q j g w u", j=UNIT, g=PASSES, u=2
+            )
+            for j in range(UNIT):
+                bank = t_psum.tile([P, BANK], F32, name="x_bank", tag="t")
+                transpose_rows(bank, x_raw[n * UNIT + j][:].bitcast(F32))
+                nc.scalar.copy(out=grouped_words[:, j], in_=words_side_by_side(bank))
+
+        def quantise_x(n):
+            width = UNIT * PASSES * P
+            x_codes[n] = xq_pool.tile([P, width], U32, name="x_codes", tag="xc", align_bytes=64)
+            x_scales[n] = xq_pool.tile([P, width], U8, name="x_scales", tag="xs", align_bytes=64)
+            nc.vector.quantize_mx(
+                out=x_codes[n][:].bitcast(FP8X4), scales=x_scales[n][:], in_=x_grouped[n][:]
+            )
+
+        hw_grouped = {}
+        hw_codes = {}
+        hw_scales = {}
+        h_banks = {}
+        o_banks = {}
+
+        def project(n):
+            h_banks[n] = []
+            for j in range(UNIT):
+                h_bank = h_psum.tile([P, BANK], F32, name="h_bank", tag="h")
+                h_banks[n].append(h_bank)
+                for c in range(PACK):
+                    for g in range(PASSES):
+                        a_cols = slice((c * PASSES + g) * P, (c * PASSES + g + 1) * P)
+                        x_cols = slice((j * PASSES + g) * P, (j * PASSES + g + 1) * P)
+                        nc.tensor.matmul_mx(
+                            out=h_bank[:, c * P : (c + 1) * P],
+                            lhsT=a_codes[:, a_cols].bitcast(FP8X4),
+                            lhsT_scale=a_scales[:, a_cols],
+                            rhs=x_codes[n][:, x_cols].bitcast(FP8X4),
+                            rhs_scale=x_scales[n][:, x_cols],
+                            start=(g == 0),
+                            stop=(g == PASSES - 1),
+                        )
+
+        def gate_h(n):
+            hw_grouped[n] = hwg_pool.tile([P, UNIT * ER], BF16, name="hw_grouped", tag="hwg", align_bytes=64)
+            for j in range(UNIT):
+                nc.vector.tensor_tensor(
+                    out=hw_grouped[n][:, j * ER : (j + 1) * ER].rearrange("q (w c) -> q w c", c=PACK),
+                    in0=h_banks[n][j][:].rearrange("q (c w) -> q w c", c=PACK),
+                    in1=route_t[n][:, j * P : (j + 1) * P].unsqueeze(2).to_broadcast([P, P, PACK]),
+                    op=ALU.mult,
+                )
+
+        def quantise_hw(n):
+            hw_codes[n] = hwq_pool.tile([P, UNIT * P], U32, name="hw_codes", tag="hc", align_bytes=64)
+            hw_scales[n] = hwq_pool.tile([P, UNIT * P], U8, name="hw_scales", tag="hs", align_bytes=64)
+            nc.vector.quantize_mx(
+                out=hw_codes[n][:].bitcast(FP8X4), scales=hw_scales[n][:], in_=hw_grouped[n][:]
+            )
+
+        def emit_output(n):
+            o_banks[n] = o_psum.tile([P, BANK], F32, name="o_bank", tag="o")
+            for j in range(UNIT):
+                o_cols = slice(j * O, (j + 1) * O)
+                for g in range(PASSES):
+                    x_cols = slice((j * PASSES + g) * P, (j * PASSES + g + 1) * P)
+                    nc.tensor.matmul_mx(
+                        out=o_banks[n][:, o_cols],
+                        lhsT=x_codes[n][:, x_cols].bitcast(FP8X4),
+                        lhsT_scale=x_scales[n][:, x_cols],
+                        rhs=w_codes[:, g * O : (g + 1) * O].bitcast(FP8X4),
+                        rhs_scale=w_scales[:, g * O : (g + 1) * O],
+                        start=(g == 0),
+                        stop=False,
+                    )
+                nc.tensor.matmul_mx(
+                    out=o_banks[n][:, o_cols],
+                    lhsT=hw_codes[n][:, j * P : (j + 1) * P].bitcast(FP8X4),
+                    lhsT_scale=hw_scales[n][:, j * P : (j + 1) * P],
+                    rhs=b_codes[:].bitcast(FP8X4),
+                    rhs_scale=b_scales[:],
+                    start=False,
+                    stop=True,
+                )
+
+        def add_bias_and_store(n):
+            o_stage = stage_pool.tile([P, UNIT * O], F32, name="o_stage", tag="os")
+            nc.vector.tensor_tensor(
+                out=o_stage[:].rearrange("p (j o) -> p j o", o=O),
+                in0=o_banks[n][:].rearrange("p (j o) -> p j o", o=O),
+                in1=bias_sb[:].unsqueeze(1).to_broadcast([P, UNIT, O]),
+                op=ALU.add,
+            )
+            nc.sync.dma_start(
+                out=out_view[:, n * UNIT : (n + 1) * UNIT, :],
+                in_=o_stage[:].rearrange("p (j o) -> p j o", o=O),
+            )
+
+        warm = keep.tile([P, 1], F32)
+        nc.vector.memset(warm[:], 0.0)
+        nc.scalar.activation(out=warm[:], in_=warm[:], func=ACT.Exp)
+
+        head = 2 * UNIT
+        softmax_shift(0, head)
+        softmax_exp_norm(0, head)
+        softmax_shift(head, SLOTS)
+        expand_route(0)
+        expand_route(1)
+        for c in range(PACK):
+            prepare_a_chunk(c)
+        transpose_route(0)
+        transpose_x(0)
+        quantise_x(0)
+        softmax_exp_norm(head, SLOTS)
+
+        for n in range(UNITS + LAG):
+            if n + 1 < UNITS:
+                transpose_route(n + 1)
+                transpose_x(n + 1)
+            if n + 2 < UNITS:
+                expand_route(n + 2)
+            if n + 2 == LAG:
+                transpose_w()
+            if n + 1 == LAG:
+                transpose_b()
+            if n < UNITS:
+                project(n)
+            if n >= LAG:
+                emit_output(n - LAG)
+            if n < UNITS:
+                gate_h(n)
+            if n + 1 < UNITS:
+                quantise_x(n + 1)
+            if n >= LAG:
+                add_bias_and_store(n - LAG)
+            if n < UNITS:
+                quantise_hw(n)
+            if n + 3 == LAG:
+                sort_b()
+            if n + 2 == LAG:
+                quantise_w()
+            if n + 1 == LAG:
+                quantise_b()

@@ -28,7 +28,12 @@ SLOTS = TOKENS // P
 UNIT = 2
 UNITS = SLOTS // UNIT
 O_TILES = O // P
-LAG = 4
+LAG = 2
+QUICK = 4
+HEAD = 16
+GROUP = P // E
+PARK = 28
+FIRST_SORTED = 6
 
 FLOPS = 2 * TOKENS * D * (O + ER) + 2 * TOKENS * ER * O
 
@@ -45,6 +50,7 @@ def tile_linearmoloralayer_pa_t_kernel(tc, x, gate_logits, W_base, b_base, A, B,
 
     with ExitStack() as ctx:
         keep = ctx.enter_context(tc.tile_pool(name="keep", bufs=1))
+        sort_pool = ctx.enter_context(tc.tile_pool(name="sort_pool", bufs=2))
         xg_pool = ctx.enter_context(tc.tile_pool(name="xg_pool", bufs=2))
         xq_pool = ctx.enter_context(tc.tile_pool(name="xq_pool", bufs=LAG + 2))
         route_pool = ctx.enter_context(tc.tile_pool(name="route_pool", bufs=2))
@@ -71,14 +77,15 @@ def tile_linearmoloralayer_pa_t_kernel(tc, x, gate_logits, W_base, b_base, A, B,
                 nc.sync.dma_start(out=x_raw[s][:], in_=x_view[:, s, :])
 
         nc.sync.dma_start(out=gate_sb[:], in_=gate_view)
+        load_x(0, UNIT)
         for c in range(PACK):
             nc.sync.dma_start(out=a_raw[c][:], in_=a_view[:, c, :])
-        load_x(0, LAG * UNIT)
+        load_x(UNIT, 2 * UNIT)
         nc.sync.dma_start(out=w_raw[:].rearrange("m (h d) -> m h d", h=O_TILES), in_=w_view)
         nc.sync.dma_start(out=b_raw[:].rearrange("m (e f) -> m e f", e=E), in_=b_view)
-        load_x(LAG * UNIT, 2 * LAG * UNIT)
+        load_x(2 * UNIT, 8 * UNIT)
         nc.sync.dma_start(out=bias_sb[:], in_=b_base.partition_broadcast(P))
-        load_x(2 * LAG * UNIT, SLOTS)
+        load_x(8 * UNIT, SLOTS)
 
         def transpose_rows(bank, words):
             for g in range(PASSES):
@@ -86,6 +93,11 @@ def tile_linearmoloralayer_pa_t_kernel(tc, x, gate_logits, W_base, b_base, A, B,
                     cols = slice((g * 2 + u) * P, (g * 2 + u + 1) * P)
                     every_second = slice(g * 2 * P + u, (g + 1) * 2 * P, 2)
                     nc.tensor.transpose(out=bank[:, cols], in_=words[:, every_second], identity=ident[:])
+
+        def transpose_sorted_rows(bank, words):
+            for block in range(WORDS // P):
+                cols = slice(block * P, (block + 1) * P)
+                nc.tensor.transpose(out=bank[:, cols], in_=words[:, cols], identity=ident[:])
 
         def words_side_by_side(bank):
             return bank[:].rearrange("q (g u m) -> q g m u", g=PASSES, u=2)
@@ -100,11 +112,14 @@ def tile_linearmoloralayer_pa_t_kernel(tc, x, gate_logits, W_base, b_base, A, B,
         def by_slot(ap):
             return ap.rearrange("p (s e) -> p s e", e=E)
 
-        def softmax_shift(first, last):
+        def softmax_max(first, last):
             cols = slice(first * E, last * E)
             nc.vector.tensor_reduce(
                 out=g_max[:, first:last], in_=by_slot(gate_sb[:, cols]), axis=AXIS.X, op=ALU.max
             )
+
+        def softmax_shift(first, last):
+            cols = slice(first * E, last * E)
             nc.vector.tensor_tensor(
                 out=by_slot(g_exp[:, cols]),
                 in0=by_slot(gate_sb[:, cols]),
@@ -112,9 +127,12 @@ def tile_linearmoloralayer_pa_t_kernel(tc, x, gate_logits, W_base, b_base, A, B,
                 op=ALU.subtract,
             )
 
-        def softmax_exp_norm(first, last):
+        def softmax_exp(first, last):
             cols = slice(first * E, last * E)
             nc.scalar.activation(out=g_exp[:, cols], in_=g_exp[:, cols], func=ACT.Exp)
+
+        def softmax_sum(first, last):
+            cols = slice(first * E, last * E)
             nc.vector.tensor_reduce(
                 out=g_sum[:, first:last], in_=by_slot(g_exp[:, cols]), axis=AXIS.X, op=ALU.add
             )
@@ -124,13 +142,24 @@ def tile_linearmoloralayer_pa_t_kernel(tc, x, gate_logits, W_base, b_base, A, B,
             first = n * UNIT
             wide = route_pool.tile([P, UNIT * P], F32, name="route_wide", tag="route_wide")
             route_wide[n] = wide
-            shape = [P, UNIT, E, PACK]
-            nc.gpsimd.tensor_tensor(
-                out=wide[:].rearrange("p (j e i) -> p j e i", j=UNIT, i=PACK),
-                in0=by_slot(g_exp[:, first * E : (first + UNIT) * E]).unsqueeze(3).to_broadcast(shape),
-                in1=g_inv[:, first : first + UNIT].unsqueeze(2).unsqueeze(3).to_broadcast(shape),
-                op=ALU.mult,
-            )
+            if n == 0:
+                shape = [P, UNIT, E, PACK]
+                nc.vector.tensor_tensor(
+                    out=wide[:].rearrange("p (j e i) -> p j e i", j=UNIT, i=PACK),
+                    in0=by_slot(g_exp[:, first * E : (first + UNIT) * E]).unsqueeze(3).to_broadcast(shape),
+                    in1=g_inv[:, first : first + UNIT].unsqueeze(2).unsqueeze(3).to_broadcast(shape),
+                    op=ALU.mult,
+                )
+                return
+            for slot in range(first, first + UNIT):
+                nc.scalar.activation(
+                    out=wide[:, (slot - first) * P : (slot - first + 1) * P].rearrange(
+                        "p (e i) -> p e i", i=PACK
+                    ),
+                    in_=g_exp[:, slot * E : (slot + 1) * E].unsqueeze(2).to_broadcast([P, E, PACK]),
+                    func=ACT.Copy,
+                    scale=g_inv[:, slot : slot + 1],
+                )
 
         def transpose_route(n):
             bank = t_psum.tile([P, UNIT * P], F32, name="route_bank", tag="t")
@@ -139,6 +168,55 @@ def tile_linearmoloralayer_pa_t_kernel(tc, x, gate_logits, W_base, b_base, A, B,
                 nc.tensor.transpose(out=bank[:, cols], in_=route_wide[n][:, cols], identity=ident[:])
             route_t[n] = route_pool.tile([P, UNIT * P], F32, name="route_t", tag="route_t")
             nc.scalar.mul(out=route_t[n][:], in_=bank[:], mul=SCALING)
+
+        def route_columns(n, j):
+            slot = n * UNIT + j
+            if slot < HEAD:
+                return route_t[n][:, j * P : (j + 1) * P]
+            group, a = divmod(slot - HEAD, GROUP)
+            first = a * REST_COLS + group * P
+            return route_rest[:, first : first + P]
+
+        REST = SLOTS - HEAD
+        GROUPS = REST // GROUP
+        REST_COLS = GROUPS * P
+        route_norm = keep.tile([P, REST * E], F32)
+        route_turned = keep.tile([P, REST_COLS], F32)
+        route_rest = keep.tile([P, GROUP * REST_COLS], F32)
+        parked = out_view[:, PARK : PARK + REST_COLS // O, :].rearrange("p s o -> p (s o)")
+
+        def normalise_rest():
+            nc.vector.tensor_tensor(
+                out=by_slot(route_norm[:]),
+                in0=by_slot(g_exp[:, HEAD * E :]),
+                in1=g_inv[:, HEAD:].unsqueeze(2).to_broadcast([P, REST, E]),
+                op=ALU.mult,
+            )
+
+        def turn_rest():
+            for first in range(0, GROUPS, BANK // P):
+                count = min(BANK // P, GROUPS - first)
+                bank = t_psum.tile([P, BANK], F32, name="rest_bank", tag="t")
+                for k in range(count):
+                    cols = slice((first + k) * P, (first + k + 1) * P)
+                    nc.tensor.transpose(
+                        out=bank[:, k * P : (k + 1) * P], in_=route_norm[:, cols], identity=ident[:]
+                    )
+                nc.scalar.mul(
+                    out=route_turned[:, first * P : (first + count) * P],
+                    in_=bank[:, : count * P],
+                    mul=SCALING,
+                )
+
+        def park_rest():
+            nc.sync.dma_start(out=parked, in_=route_turned[:])
+
+        def fetch_rest():
+            for i in range(P // E):
+                nc.sync.dma_start(
+                    out=route_rest[i : P : P // E, :].rearrange("e (a n) -> e a n", a=GROUP),
+                    in_=parked.rearrange("(a e) n -> e a n", a=GROUP),
+                )
 
         a_grouped = keep.tile([P, PACK * D], BF16, align_bytes=64)
         a_codes = keep.tile([P, PACK * PASSES * P], U32, align_bytes=64)
@@ -151,13 +229,15 @@ def tile_linearmoloralayer_pa_t_kernel(tc, x, gate_logits, W_base, b_base, A, B,
         b_codes = keep.tile([P, O], U32, align_bytes=64)
         b_scales = keep.tile([P, O], U8, align_bytes=64)
 
-        def prepare_a_chunk(c):
+        def transpose_a(c):
             bank = t_psum.tile([P, BANK], F32, name="a_bank", tag="t")
             transpose_rows(bank, a_raw[c][:].bitcast(F32))
             grouped_words = a_grouped[:].bitcast(F32).rearrange(
                 "q (c g m u) -> q c g m u", c=PACK, g=PASSES, u=2
             )
             nc.scalar.copy(out=grouped_words[:, c], in_=words_side_by_side(bank))
+
+        def quantise_a(c):
             cols = slice(c * PASSES * P, (c + 1) * PASSES * P)
             nc.vector.quantize_mx(
                 out=a_codes[:, cols].bitcast(FP8X4),
@@ -202,9 +282,23 @@ def tile_linearmoloralayer_pa_t_kernel(tc, x, gate_logits, W_base, b_base, A, B,
                 out=b_codes[:].bitcast(FP8X4), scales=b_scales[:], in_=b_grouped[:]
             )
 
+        x_sorted = {}
         x_grouped = {}
         x_codes = {}
         x_scales = {}
+
+        def sort_x(n):
+            x_sorted[n] = sort_pool.tile([P, UNIT * D], BF16, name="x_sorted", tag="xsort", align_bytes=64)
+            words = x_sorted[n][:].bitcast(F32)
+            for j in range(UNIT):
+                nc.scalar.copy(
+                    out=words[:, j * WORDS : (j + 1) * WORDS].rearrange(
+                        "p (g u q) -> p g u q", g=PASSES, u=2
+                    ),
+                    in_=x_raw[n * UNIT + j][:].bitcast(F32).rearrange(
+                        "p (g q u) -> p g u q", g=PASSES, u=2
+                    ),
+                )
 
         def transpose_x(n):
             x_grouped[n] = xg_pool.tile([P, UNIT * D], BF16, name="x_grouped", tag="xg", align_bytes=64)
@@ -213,7 +307,11 @@ def tile_linearmoloralayer_pa_t_kernel(tc, x, gate_logits, W_base, b_base, A, B,
             )
             for j in range(UNIT):
                 bank = t_psum.tile([P, BANK], F32, name="x_bank", tag="t")
-                transpose_rows(bank, x_raw[n * UNIT + j][:].bitcast(F32))
+                if n < FIRST_SORTED:
+                    transpose_rows(bank, x_raw[n * UNIT + j][:].bitcast(F32))
+                else:
+                    words = x_sorted[n][:].bitcast(F32)
+                    transpose_sorted_rows(bank, words[:, j * WORDS : (j + 1) * WORDS])
                 nc.scalar.copy(out=grouped_words[:, j], in_=words_side_by_side(bank))
 
         def quantise_x(n):
@@ -230,12 +328,16 @@ def tile_linearmoloralayer_pa_t_kernel(tc, x, gate_logits, W_base, b_base, A, B,
         h_banks = {}
         o_banks = {}
 
-        def project(n):
+        def open_h(n):
             h_banks[n] = []
             for j in range(UNIT):
                 h_bank = h_psum.tile([P, BANK], F32, name="h_bank", tag="h")
                 h_banks[n].append(h_bank)
-                for c in range(PACK):
+
+        def project(n, chunks):
+            for j in range(UNIT):
+                h_bank = h_banks[n][j]
+                for c in chunks:
                     for g in range(PASSES):
                         a_cols = slice((c * PASSES + g) * P, (c * PASSES + g + 1) * P)
                         x_cols = slice((j * PASSES + g) * P, (j * PASSES + g + 1) * P)
@@ -255,7 +357,7 @@ def tile_linearmoloralayer_pa_t_kernel(tc, x, gate_logits, W_base, b_base, A, B,
                 nc.vector.tensor_tensor(
                     out=hw_grouped[n][:, j * ER : (j + 1) * ER].rearrange("q (w c) -> q w c", c=PACK),
                     in0=h_banks[n][j][:].rearrange("q (c w) -> q w c", c=PACK),
-                    in1=route_t[n][:, j * P : (j + 1) * P].unsqueeze(2).to_broadcast([P, P, PACK]),
+                    in1=route_columns(n, j).unsqueeze(2).to_broadcast([P, P, PACK]),
                     op=ALU.mult,
                 )
 
@@ -308,42 +410,75 @@ def tile_linearmoloralayer_pa_t_kernel(tc, x, gate_logits, W_base, b_base, A, B,
         nc.vector.memset(warm[:], 0.0)
         nc.scalar.activation(out=warm[:], in_=warm[:], func=ACT.Exp)
 
-        head = 2 * UNIT
-        softmax_shift(0, head)
-        softmax_exp_norm(0, head)
-        softmax_shift(head, SLOTS)
-        expand_route(0)
-        expand_route(1)
-        for c in range(PACK):
-            prepare_a_chunk(c)
-        transpose_route(0)
+        softmax_max(0, QUICK)
+        softmax_shift(0, QUICK)
+        softmax_exp(0, QUICK)
+        softmax_max(QUICK, HEAD)
+        softmax_shift(QUICK, HEAD)
         transpose_x(0)
+        softmax_sum(0, QUICK)
+        expand_route(0)
         quantise_x(0)
-        softmax_exp_norm(head, SLOTS)
+        transpose_a(0)
+        transpose_a(1)
+        transpose_route(0)
+        transpose_a(2)
+        transpose_a(3)
+        for c in range(PACK):
+            quantise_a(c)
+        open_h(0)
+        project(0, (0,))
+        project(0, (1,))
+        transpose_x(1)
+        expand_route(1)
+        softmax_exp(QUICK, HEAD)
+        project(0, (2,))
+        project(0, (3,))
 
         for n in range(UNITS + LAG):
-            if n + 1 < UNITS:
-                transpose_route(n + 1)
+            if 0 < n < UNITS - 1:
                 transpose_x(n + 1)
-            if n + 2 < UNITS:
-                expand_route(n + 2)
+            if (n + 1) * UNIT < HEAD:
+                transpose_route(n + 1)
             if n + 2 == LAG:
                 transpose_w()
             if n + 1 == LAG:
                 transpose_b()
-            if n < UNITS:
-                project(n)
+            if n == 2:
+                softmax_exp(HEAD, SLOTS)
+            if n == 6:
+                turn_rest()
+                park_rest()
+                fetch_rest()
+            if 0 < n and (n + 2) * UNIT < HEAD:
+                expand_route(n + 2)
+            if FIRST_SORTED <= n + 2 < UNITS:
+                sort_x(n + 2)
+            if 0 < n < UNITS:
+                open_h(n)
+                project(n, range(PACK))
             if n >= LAG:
                 emit_output(n - LAG)
-            if n < UNITS:
-                gate_h(n)
             if n + 1 < UNITS:
                 quantise_x(n + 1)
+            if n < UNITS:
+                gate_h(n)
+            if n == 0:
+                softmax_sum(QUICK, HEAD)
+                expand_route(2)
             if n >= LAG:
                 add_bias_and_store(n - LAG)
             if n < UNITS:
                 quantise_hw(n)
-            if n + 3 == LAG:
+            if n == 0:
+                softmax_max(HEAD, SLOTS)
+            if n == 1:
+                softmax_shift(HEAD, SLOTS)
+            if n == 3:
+                softmax_sum(HEAD, SLOTS)
+            if n == 4:
+                normalise_rest()
+            if n + 2 == LAG:
                 sort_b()
             if n + 2 == LAG:
                 quantise_w()

@@ -28,8 +28,8 @@ SLOTS = TOKENS // P
 UNIT = 2
 UNITS = SLOTS // UNIT
 O_TILES = O // P
-LAG = 2
-QUICK = 4
+LAG = 3
+QUICK = 8
 HEAD = 16
 GROUP = P // E
 PARK = 28
@@ -50,10 +50,10 @@ def tile_linearmoloralayer_pa_t_kernel(tc, x, gate_logits, W_base, b_base, A, B,
 
     with ExitStack() as ctx:
         keep = ctx.enter_context(tc.tile_pool(name="keep", bufs=1))
-        sort_pool = ctx.enter_context(tc.tile_pool(name="sort_pool", bufs=2))
-        xg_pool = ctx.enter_context(tc.tile_pool(name="xg_pool", bufs=2))
+        sort_pool = ctx.enter_context(tc.tile_pool(name="sort_pool", bufs=4))
+        xg_pool = ctx.enter_context(tc.tile_pool(name="xg_pool", bufs=4))
         xq_pool = ctx.enter_context(tc.tile_pool(name="xq_pool", bufs=LAG + 2))
-        route_pool = ctx.enter_context(tc.tile_pool(name="route_pool", bufs=2))
+        route_pool = ctx.enter_context(tc.tile_pool(name="route_pool", bufs=4))
         hwg_pool = ctx.enter_context(tc.tile_pool(name="hwg_pool", bufs=2))
         hwq_pool = ctx.enter_context(tc.tile_pool(name="hwq_pool", bufs=LAG + 1))
         stage_pool = ctx.enter_context(tc.tile_pool(name="stage_pool", bufs=6))
@@ -312,7 +312,8 @@ def tile_linearmoloralayer_pa_t_kernel(tc, x, gate_logits, W_base, b_base, A, B,
                 else:
                     words = x_sorted[n][:].bitcast(F32)
                     transpose_sorted_rows(bank, words[:, j * WORDS : (j + 1) * WORDS])
-                nc.scalar.copy(out=grouped_words[:, j], in_=words_side_by_side(bank))
+                copy = nc.vector.tensor_copy if (n, j) == (0, 1) else nc.scalar.copy
+                copy(out=grouped_words[:, j], in_=words_side_by_side(bank))
 
         def quantise_x(n):
             width = UNIT * PASSES * P
@@ -413,11 +414,9 @@ def tile_linearmoloralayer_pa_t_kernel(tc, x, gate_logits, W_base, b_base, A, B,
         softmax_max(0, QUICK)
         softmax_shift(0, QUICK)
         softmax_exp(0, QUICK)
-        softmax_max(QUICK, HEAD)
-        softmax_shift(QUICK, HEAD)
-        transpose_x(0)
         softmax_sum(0, QUICK)
         expand_route(0)
+        transpose_x(0)
         quantise_x(0)
         transpose_a(0)
         transpose_a(1)
@@ -426,51 +425,57 @@ def tile_linearmoloralayer_pa_t_kernel(tc, x, gate_logits, W_base, b_base, A, B,
         transpose_a(3)
         for c in range(PACK):
             quantise_a(c)
+        softmax_max(QUICK, HEAD)
+        softmax_shift(QUICK, HEAD)
         open_h(0)
         project(0, (0,))
         project(0, (1,))
         transpose_x(1)
         expand_route(1)
-        softmax_exp(QUICK, HEAD)
         project(0, (2,))
         project(0, (3,))
+        transpose_route(1)
+        softmax_exp(QUICK, HEAD)
+        expand_route(2)
 
         for n in range(UNITS + LAG):
-            if 0 < n < UNITS - 1:
-                transpose_x(n + 1)
-            if (n + 1) * UNIT < HEAD:
-                transpose_route(n + 1)
-            if n + 2 == LAG:
-                transpose_w()
-            if n + 1 == LAG:
-                transpose_b()
-            if n == 2:
-                softmax_exp(HEAD, SLOTS)
-            if n == 6:
-                turn_rest()
-                park_rest()
-                fetch_rest()
-            if 0 < n and (n + 2) * UNIT < HEAD:
-                expand_route(n + 2)
-            if FIRST_SORTED <= n + 2 < UNITS:
-                sort_x(n + 2)
             if 0 < n < UNITS:
                 open_h(n)
                 project(n, range(PACK))
             if n >= LAG:
                 emit_output(n - LAG)
+            if n + 2 < 6:
+                transpose_x(n + 2)
+            elif (n + 2 - 6) % 2 == 0:
+                for unit in range(n + 2, min(n + 4, UNITS)):
+                    transpose_x(unit)
+            if n + 2 < HEAD // UNIT:
+                transpose_route(n + 2)
+            if n == 0:
+                transpose_w()
+            if n == 1:
+                transpose_b()
+            if n == 5:
+                turn_rest()
+                park_rest()
+                fetch_rest()
+            if n == 2:
+                softmax_exp(HEAD, SLOTS)
+            if n + 3 < HEAD // UNIT:
+                expand_route(n + 3)
+            if FIRST_SORTED <= n + 4 < UNITS:
+                sort_x(n + 4)
             if n + 1 < UNITS:
                 quantise_x(n + 1)
             if n < UNITS:
                 gate_h(n)
-            if n == 0:
-                softmax_sum(QUICK, HEAD)
-                expand_route(2)
             if n >= LAG:
                 add_bias_and_store(n - LAG)
             if n < UNITS:
                 quantise_hw(n)
             if n == 0:
+                softmax_sum(QUICK, HEAD)
+            if n == 1:
                 softmax_max(HEAD, SLOTS)
             if n == 1:
                 softmax_shift(HEAD, SLOTS)
@@ -478,9 +483,9 @@ def tile_linearmoloralayer_pa_t_kernel(tc, x, gate_logits, W_base, b_base, A, B,
                 softmax_sum(HEAD, SLOTS)
             if n == 4:
                 normalise_rest()
-            if n + 2 == LAG:
+            if n == 0:
                 sort_b()
-            if n + 2 == LAG:
+            if n == 1:
                 quantise_w()
-            if n + 1 == LAG:
+            if n == 2:
                 quantise_b()

@@ -76,14 +76,16 @@ def tile_linearmoloralayer_pa_t_kernel(tc, x, gate_logits, W_base, b_base, A, B,
             for s in range(first, last):
                 nc.sync.dma_start(out=x_raw[s][:], in_=x_view[:, s, :])
 
-        nc.sync.dma_start(out=gate_sb[:], in_=gate_view)
+        nc.sync.dma_start(out=gate_sb[:, : QUICK * E], in_=gate_view[:, : QUICK * E])
         load_x(0, UNIT)
         for c in range(PACK):
             nc.sync.dma_start(out=a_raw[c][:], in_=a_view[:, c, :])
         load_x(UNIT, 2 * UNIT)
+        nc.sync.dma_start(out=gate_sb[:, QUICK * E :], in_=gate_view[:, QUICK * E :])
+        load_x(2 * UNIT, 3 * UNIT)
         nc.sync.dma_start(out=w_raw[:].rearrange("m (h d) -> m h d", h=O_TILES), in_=w_view)
         nc.sync.dma_start(out=b_raw[:].rearrange("m (e f) -> m e f", e=E), in_=b_view)
-        load_x(2 * UNIT, 8 * UNIT)
+        load_x(3 * UNIT, 8 * UNIT)
         nc.sync.dma_start(out=bias_sb[:], in_=b_base.partition_broadcast(P))
         load_x(8 * UNIT, SLOTS)
 
@@ -260,13 +262,16 @@ def tile_linearmoloralayer_pa_t_kernel(tc, x, gate_logits, W_base, b_base, A, B,
             )
 
         def sort_b():
-            nc.vector.tensor_copy(
-                out=b_sorted[:].rearrange("m (h e r) -> m h e r", h=O_TILES, r=RANK),
-                in_=b_raw[:].rearrange("m (e h r) -> m h e r", h=O_TILES, r=RANK),
-            )
+            for h in range(O_TILES):
+                nc.scalar.copy(
+                    out=b_sorted[:].bitcast(F32)[:, h * ER // 2 : (h + 1) * ER // 2].rearrange(
+                        "m (u e v) -> m e v u", u=2, e=E
+                    ),
+                    in_=b_raw[:].bitcast(F32).rearrange("m (e h v u) -> m h e v u", h=O_TILES, e=E, u=2)[:, h],
+                )
 
         def transpose_b():
-            words = b_sorted[:].bitcast(F32).rearrange("m (h q u) -> m h u q", h=O_TILES, u=2)
+            words = b_sorted[:].bitcast(F32).rearrange("m (h u q) -> m h u q", h=O_TILES, u=2)
             bank = t_psum.tile([P, BANK], F32, name="b_bank", tag="t")
             for h in range(O_TILES):
                 for u in range(2):
@@ -327,7 +332,8 @@ def tile_linearmoloralayer_pa_t_kernel(tc, x, gate_logits, W_base, b_base, A, B,
         hw_codes = {}
         hw_scales = {}
         h_banks = {}
-        o_banks = {}
+        o_slots = {}
+        o_pieces = {}
 
         def open_h(n):
             h_banks[n] = []
@@ -370,13 +376,22 @@ def tile_linearmoloralayer_pa_t_kernel(tc, x, gate_logits, W_base, b_base, A, B,
             )
 
         def emit_output(n):
-            o_banks[n] = o_psum.tile([P, BANK], F32, name="o_bank", tag="o")
+            if n < UNITS - 1:
+                bank = o_psum.tile([P, BANK], F32, name="o_bank", tag="o")
+                o_slots[n] = [bank[:, j * O : (j + 1) * O] for j in range(UNIT)]
+                o_pieces[n] = [(0, UNIT, bank[:])]
+            else:
+                o_slots[n] = []
+                o_pieces[n] = []
+                for j in range(UNIT):
+                    bank = t_psum.tile([P, BANK], F32, name="o_last", tag="t")
+                    o_slots[n].append(bank[:, :O])
+                    o_pieces[n].append((j, 1, bank[:, :O]))
             for j in range(UNIT):
-                o_cols = slice(j * O, (j + 1) * O)
                 for g in range(PASSES):
                     x_cols = slice((j * PASSES + g) * P, (j * PASSES + g + 1) * P)
                     nc.tensor.matmul_mx(
-                        out=o_banks[n][:, o_cols],
+                        out=o_slots[n][j],
                         lhsT=x_codes[n][:, x_cols].bitcast(FP8X4),
                         lhsT_scale=x_scales[n][:, x_cols],
                         rhs=w_codes[:, g * O : (g + 1) * O].bitcast(FP8X4),
@@ -385,7 +400,7 @@ def tile_linearmoloralayer_pa_t_kernel(tc, x, gate_logits, W_base, b_base, A, B,
                         stop=False,
                     )
                 nc.tensor.matmul_mx(
-                    out=o_banks[n][:, o_cols],
+                    out=o_slots[n][j],
                     lhsT=hw_codes[n][:, j * P : (j + 1) * P].bitcast(FP8X4),
                     lhsT_scale=hw_scales[n][:, j * P : (j + 1) * P],
                     rhs=b_codes[:].bitcast(FP8X4),
@@ -396,16 +411,16 @@ def tile_linearmoloralayer_pa_t_kernel(tc, x, gate_logits, W_base, b_base, A, B,
 
         def add_bias_and_store(n):
             o_stage = stage_pool.tile([P, UNIT * O], F32, name="o_stage", tag="os")
-            nc.vector.tensor_tensor(
-                out=o_stage[:].rearrange("p (j o) -> p j o", o=O),
-                in0=o_banks[n][:].rearrange("p (j o) -> p j o", o=O),
-                in1=bias_sb[:].unsqueeze(1).to_broadcast([P, UNIT, O]),
-                op=ALU.add,
-            )
-            nc.sync.dma_start(
-                out=out_view[:, n * UNIT : (n + 1) * UNIT, :],
-                in_=o_stage[:].rearrange("p (j o) -> p j o", o=O),
-            )
+            for first, count, piece in o_pieces[n]:
+                staged = o_stage[:, first * O : (first + count) * O].rearrange("p (j o) -> p j o", o=O)
+                nc.vector.tensor_tensor(
+                    out=staged,
+                    in0=piece.rearrange("p (j o) -> p j o", o=O),
+                    in1=bias_sb[:].unsqueeze(1).to_broadcast([P, count, O]),
+                    op=ALU.add,
+                )
+                slot = n * UNIT + first
+                nc.sync.dma_start(out=out_view[:, slot : slot + count, :], in_=staged)
 
         warm = keep.tile([P, 1], F32)
         nc.vector.memset(warm[:], 0.0)

@@ -30,7 +30,7 @@ UNITS = SLOTS // UNIT
 O_TILES = O // P
 LAG = 3
 QUICK = 8
-HEAD = 16
+HEAD = 12
 GROUP = P // E
 PARK = 28
 FIRST_SORTED = 6
@@ -85,9 +85,8 @@ def tile_linearmoloralayer_pa_t_kernel(tc, x, gate_logits, W_base, b_base, A, B,
         load_x(2 * UNIT, 3 * UNIT)
         nc.sync.dma_start(out=w_raw[:].rearrange("m (h d) -> m h d", h=O_TILES), in_=w_view)
         nc.sync.dma_start(out=b_raw[:].rearrange("m (e f) -> m e f", e=E), in_=b_view)
-        load_x(3 * UNIT, 8 * UNIT)
+        load_x(3 * UNIT, 10 * UNIT)
         nc.sync.dma_start(out=bias_sb[:], in_=b_base.partition_broadcast(P))
-        load_x(8 * UNIT, SLOTS)
 
         def transpose_rows(bank, words):
             for g in range(PASSES):
@@ -122,7 +121,8 @@ def tile_linearmoloralayer_pa_t_kernel(tc, x, gate_logits, W_base, b_base, A, B,
 
         def softmax_shift(first, last):
             cols = slice(first * E, last * E)
-            nc.vector.tensor_tensor(
+            engine = nc.vector if first == 0 else nc.vector
+            engine.tensor_tensor(
                 out=by_slot(g_exp[:, cols]),
                 in0=by_slot(gate_sb[:, cols]),
                 in1=g_max[:, first:last].unsqueeze(2).to_broadcast([P, last - first, E]),
@@ -185,7 +185,7 @@ def tile_linearmoloralayer_pa_t_kernel(tc, x, gate_logits, W_base, b_base, A, B,
         route_norm = keep.tile([P, REST * E], F32)
         route_turned = keep.tile([P, REST_COLS], F32)
         route_rest = keep.tile([P, GROUP * REST_COLS], F32)
-        parked = out_view[:, PARK : PARK + REST_COLS // O, :].rearrange("p s o -> p (s o)")
+        parked = out_view[:, PARK:, :].rearrange("p s o -> p (s o)")[:, :REST_COLS]
 
         def normalise_rest():
             nc.vector.tensor_tensor(
@@ -338,7 +338,10 @@ def tile_linearmoloralayer_pa_t_kernel(tc, x, gate_logits, W_base, b_base, A, B,
         def open_h(n):
             h_banks[n] = []
             for j in range(UNIT):
-                h_bank = h_psum.tile([P, BANK], F32, name="h_bank", tag="h")
+                if n < UNITS - 1:
+                    h_bank = h_psum.tile([P, BANK], F32, name="h_bank", tag="h")
+                else:
+                    h_bank = t_psum.tile([P, BANK], F32, name="h_last", tag="t")
                 h_banks[n].append(h_bank)
 
         def project(n, chunks):
@@ -377,7 +380,10 @@ def tile_linearmoloralayer_pa_t_kernel(tc, x, gate_logits, W_base, b_base, A, B,
 
         def emit_output(n):
             if n < UNITS - 1:
-                bank = o_psum.tile([P, BANK], F32, name="o_bank", tag="o")
+                if n < UNITS - 2:
+                    bank = o_psum.tile([P, BANK], F32, name="o_bank", tag="o")
+                else:
+                    bank = h_psum.tile([P, BANK], F32, name="o_late", tag="h")
                 o_slots[n] = [bank[:, j * O : (j + 1) * O] for j in range(UNIT)]
                 o_pieces[n] = [(0, UNIT, bank[:])]
             else:
@@ -440,18 +446,18 @@ def tile_linearmoloralayer_pa_t_kernel(tc, x, gate_logits, W_base, b_base, A, B,
         transpose_a(3)
         for c in range(PACK):
             quantise_a(c)
-        softmax_max(QUICK, HEAD)
-        softmax_shift(QUICK, HEAD)
+        softmax_max(QUICK, SLOTS)
+        softmax_shift(QUICK, SLOTS)
+        expand_route(1)
+        expand_route(2)
         open_h(0)
         project(0, (0,))
         project(0, (1,))
         transpose_x(1)
-        expand_route(1)
+        transpose_route(1)
         project(0, (2,))
         project(0, (3,))
-        transpose_route(1)
-        softmax_exp(QUICK, HEAD)
-        expand_route(2)
+        softmax_exp(QUICK, SLOTS)
 
         for n in range(UNITS + LAG):
             if 0 < n < UNITS:
@@ -466,16 +472,15 @@ def tile_linearmoloralayer_pa_t_kernel(tc, x, gate_logits, W_base, b_base, A, B,
                     transpose_x(unit)
             if n + 2 < HEAD // UNIT:
                 transpose_route(n + 2)
-            if n == 0:
+            if n == 1:
                 transpose_w()
             if n == 1:
                 transpose_b()
-            if n == 5:
+            if n == 2:
                 turn_rest()
                 park_rest()
                 fetch_rest()
-            if n == 2:
-                softmax_exp(HEAD, SLOTS)
+                load_x(10 * UNIT, SLOTS)
             if n + 3 < HEAD // UNIT:
                 expand_route(n + 3)
             if FIRST_SORTED <= n + 4 < UNITS:
@@ -489,18 +494,12 @@ def tile_linearmoloralayer_pa_t_kernel(tc, x, gate_logits, W_base, b_base, A, B,
             if n < UNITS:
                 quantise_hw(n)
             if n == 0:
-                softmax_sum(QUICK, HEAD)
+                softmax_sum(QUICK, SLOTS)
             if n == 1:
-                softmax_max(HEAD, SLOTS)
-            if n == 1:
-                softmax_shift(HEAD, SLOTS)
-            if n == 3:
-                softmax_sum(HEAD, SLOTS)
-            if n == 4:
                 normalise_rest()
             if n == 0:
                 sort_b()
-            if n == 1:
+            if n == 2:
                 quantise_w()
             if n == 2:
                 quantise_b()

@@ -30,10 +30,9 @@ UNITS = SLOTS // UNIT
 O_TILES = O // P
 LAG = 3
 QUICK = 8
-HEAD = 12
+HEAD = 8
 GROUP = P // E
-PARK = 28
-FIRST_SORTED = 6
+FIRST_SORTED = 5
 
 FLOPS = 2 * TOKENS * D * (O + ER) + 2 * TOKENS * ER * O
 
@@ -185,7 +184,6 @@ def tile_linearmoloralayer_pa_t_kernel(tc, x, gate_logits, W_base, b_base, A, B,
         route_norm = keep.tile([P, REST * E], F32)
         route_turned = keep.tile([P, REST_COLS], F32)
         route_rest = keep.tile([P, GROUP * REST_COLS], F32)
-        parked = out_view[:, PARK:, :].rearrange("p s o -> p (s o)")[:, :REST_COLS]
 
         def normalise_rest():
             nc.vector.tensor_tensor(
@@ -210,15 +208,13 @@ def tile_linearmoloralayer_pa_t_kernel(tc, x, gate_logits, W_base, b_base, A, B,
                     mul=SCALING,
                 )
 
-        def park_rest():
-            nc.sync.dma_start(out=parked, in_=route_turned[:])
-
-        def fetch_rest():
-            for i in range(P // E):
-                nc.sync.dma_start(
-                    out=route_rest[i : P : P // E, :].rearrange("e (a n) -> e a n", a=GROUP),
-                    in_=parked.rearrange("(a e) n -> e a n", a=GROUP),
-                )
+        def spread_rest():
+            for a in range(GROUP):
+                for i in range(P // E):
+                    nc.sync.dma_start(
+                        out=route_rest[i : P : P // E, a * REST_COLS : (a + 1) * REST_COLS],
+                        in_=route_turned[a * E : (a + 1) * E, :],
+                    )
 
         a_grouped = keep.tile([P, PACK * D], BF16, align_bytes=64)
         a_codes = keep.tile([P, PACK * PASSES * P], U32, align_bytes=64)
@@ -338,7 +334,9 @@ def tile_linearmoloralayer_pa_t_kernel(tc, x, gate_logits, W_base, b_base, A, B,
         def open_h(n):
             h_banks[n] = []
             for j in range(UNIT):
-                if n < UNITS - 1:
+                if n == 1:
+                    h_bank = o_psum.tile([P, BANK], F32, name="h_early", tag="o")
+                elif n < UNITS - 1:
                     h_bank = h_psum.tile([P, BANK], F32, name="h_bank", tag="h")
                 else:
                     h_bank = t_psum.tile([P, BANK], F32, name="h_last", tag="t")
@@ -476,10 +474,9 @@ def tile_linearmoloralayer_pa_t_kernel(tc, x, gate_logits, W_base, b_base, A, B,
                 transpose_w()
             if n == 1:
                 transpose_b()
-            if n == 2:
+            if n == 1:
                 turn_rest()
-                park_rest()
-                fetch_rest()
+                spread_rest()
                 load_x(10 * UNIT, SLOTS)
             if n + 3 < HEAD // UNIT:
                 expand_route(n + 3)
@@ -495,7 +492,7 @@ def tile_linearmoloralayer_pa_t_kernel(tc, x, gate_logits, W_base, b_base, A, B,
                 quantise_hw(n)
             if n == 0:
                 softmax_sum(QUICK, SLOTS)
-            if n == 1:
+            if n == 0:
                 normalise_rest()
             if n == 0:
                 sort_b()

@@ -448,6 +448,7 @@ def tile_linearmoloralayer_pa_t_kernel(tc, x, gate_logits, W_base, b_base, A, B,
         softmax_shift(QUICK, SLOTS)
         expand_route(1)
         expand_route(2)
+        expand_route(3)
         open_h(0)
         project(0, (0,))
         project(0, (1,))
@@ -460,26 +461,34 @@ def tile_linearmoloralayer_pa_t_kernel(tc, x, gate_logits, W_base, b_base, A, B,
         for n in range(UNITS + LAG):
             if 0 < n < UNITS:
                 open_h(n)
-                project(n, range(PACK))
+                if n == 1:
+                    project(n, (0, 1))
+                    transpose_w()
+                    project(n, (2, 3))
+                elif n == 2:
+                    project(n, (0, 1))
+                    transpose_b()
+                    project(n, (2, 3))
+                else:
+                    project(n, range(PACK))
             if n >= LAG:
                 emit_output(n - LAG)
-            if n + 2 < 6:
-                transpose_x(n + 2)
-            elif (n + 2 - 6) % 2 == 0:
+            if n == 0:
+                transpose_x(2)
+                transpose_route(2)
+            if n == 1:
+                transpose_x(3)
+                transpose_route(3)
+                turn_rest()
+            if n == 2:
+                transpose_x(4)
+                transpose_x(5)
+            if n >= 4 and n % 2 == 0:
                 for unit in range(n + 2, min(n + 4, UNITS)):
                     transpose_x(unit)
-            if n + 2 < HEAD // UNIT:
-                transpose_route(n + 2)
             if n == 1:
-                transpose_w()
-            if n == 1:
-                transpose_b()
-            if n == 1:
-                turn_rest()
                 spread_rest()
                 load_x(10 * UNIT, SLOTS)
-            if n + 3 < HEAD // UNIT:
-                expand_route(n + 3)
             if FIRST_SORTED <= n + 4 < UNITS:
                 sort_x(n + 4)
             if n + 1 < UNITS:

@@ -54,7 +54,7 @@ def tile_linearmoloralayer_pa_t_kernel(tc, x, gate_logits, W_base, b_base, A, B,
         xq_pool = ctx.enter_context(tc.tile_pool(name="xq_pool", bufs=LAG + 2))
         route_pool = ctx.enter_context(tc.tile_pool(name="route_pool", bufs=4))
         hwg_pool = ctx.enter_context(tc.tile_pool(name="hwg_pool", bufs=2))
-        hwq_pool = ctx.enter_context(tc.tile_pool(name="hwq_pool", bufs=LAG + 1))
+        hwq_pool = ctx.enter_context(tc.tile_pool(name="hwq_pool", bufs=LAG))
         stage_pool = ctx.enter_context(tc.tile_pool(name="stage_pool", bufs=6))
         t_psum = ctx.enter_context(tc.psum_pool(name="t_psum", bufs=4))
         h_psum = ctx.enter_context(tc.psum_pool(name="h_psum", bufs=2))
@@ -84,7 +84,7 @@ def tile_linearmoloralayer_pa_t_kernel(tc, x, gate_logits, W_base, b_base, A, B,
         load_x(2 * UNIT, 3 * UNIT)
         nc.sync.dma_start(out=w_raw[:].rearrange("m (h d) -> m h d", h=O_TILES), in_=w_view)
         nc.sync.dma_start(out=b_raw[:].rearrange("m (e f) -> m e f", e=E), in_=b_view)
-        load_x(3 * UNIT, 10 * UNIT)
+        load_x(3 * UNIT, 9 * UNIT)
         nc.sync.dma_start(out=bias_sb[:], in_=b_base.partition_broadcast(P))
 
         def transpose_rows(bank, words):
@@ -187,9 +187,12 @@ def tile_linearmoloralayer_pa_t_kernel(tc, x, gate_logits, W_base, b_base, A, B,
 
         def normalise_rest():
             nc.vector.tensor_tensor(
-                out=by_slot(route_norm[:]),
-                in0=by_slot(g_exp[:, HEAD * E :]),
-                in1=g_inv[:, HEAD:].unsqueeze(2).to_broadcast([P, REST, E]),
+                out=route_norm[:].rearrange("p (g e a) -> p g e a", e=E, a=GROUP),
+                in0=g_exp[:, HEAD * E :].rearrange("p (g a e) -> p g e a", a=GROUP, e=E),
+                in1=g_inv[:, HEAD:]
+                .rearrange("p (g a) -> p g a", a=GROUP)
+                .unsqueeze(2)
+                .to_broadcast([P, GROUPS, E, GROUP]),
                 op=ALU.mult,
             )
 
@@ -213,7 +216,7 @@ def tile_linearmoloralayer_pa_t_kernel(tc, x, gate_logits, W_base, b_base, A, B,
                 for i in range(P // E):
                     nc.sync.dma_start(
                         out=route_rest[i : P : P // E, a * REST_COLS : (a + 1) * REST_COLS],
-                        in_=route_turned[a * E : (a + 1) * E, :],
+                        in_=route_turned[a : P : GROUP, :],
                     )
 
         a_grouped = keep.tile([P, PACK * D], BF16, align_bytes=64)
@@ -360,20 +363,33 @@ def tile_linearmoloralayer_pa_t_kernel(tc, x, gate_logits, W_base, b_base, A, B,
                         )
 
         def gate_h(n):
-            hw_grouped[n] = hwg_pool.tile([P, UNIT * ER], BF16, name="hw_grouped", tag="hwg", align_bytes=64)
+            pair, place = divmod(n + 1, 2)
+            if pair not in hw_grouped:
+                hw_grouped[pair] = hwg_pool.tile(
+                    [P, 2 * UNIT * ER], BF16, name="hw_grouped", tag="hwg", align_bytes=64
+                )
             for j in range(UNIT):
+                first = (place * UNIT + j) * ER
                 nc.vector.tensor_tensor(
-                    out=hw_grouped[n][:, j * ER : (j + 1) * ER].rearrange("q (w c) -> q w c", c=PACK),
+                    out=hw_grouped[pair][:, first : first + ER].rearrange("q (w c) -> q w c", c=PACK),
                     in0=h_banks[n][j][:].rearrange("q (c w) -> q w c", c=PACK),
                     in1=route_columns(n, j).unsqueeze(2).to_broadcast([P, P, PACK]),
                     op=ALU.mult,
                 )
 
         def quantise_hw(n):
-            hw_codes[n] = hwq_pool.tile([P, UNIT * P], U32, name="hw_codes", tag="hc", align_bytes=64)
-            hw_scales[n] = hwq_pool.tile([P, UNIT * P], U8, name="hw_scales", tag="hs", align_bytes=64)
+            if n % 2 == 1 and n < UNITS - 1:
+                return
+            pair = (n + 1) // 2
+            first = 1 if n == 0 else 0
+            last = 1 if n == UNITS - 1 else 2
+            hw_codes[pair] = hwq_pool.tile([P, 2 * UNIT * P], U32, name="hw_codes", tag="hc", align_bytes=64)
+            hw_scales[pair] = hwq_pool.tile([P, 2 * UNIT * P], U8, name="hw_scales", tag="hs", align_bytes=64)
+            cols = slice(first * UNIT * P, last * UNIT * P)
             nc.vector.quantize_mx(
-                out=hw_codes[n][:].bitcast(FP8X4), scales=hw_scales[n][:], in_=hw_grouped[n][:]
+                out=hw_codes[pair][:, cols].bitcast(FP8X4),
+                scales=hw_scales[pair][:, cols],
+                in_=hw_grouped[pair][:, first * UNIT * ER : last * UNIT * ER],
             )
 
         def emit_output(n):
@@ -403,10 +419,12 @@ def tile_linearmoloralayer_pa_t_kernel(tc, x, gate_logits, W_base, b_base, A, B,
                         start=(g == 0),
                         stop=False,
                     )
+                pair, place = divmod(n + 1, 2)
+                hw_cols = slice((place * UNIT + j) * P, (place * UNIT + j + 1) * P)
                 nc.tensor.matmul_mx(
                     out=o_slots[n][j],
-                    lhsT=hw_codes[n][:, j * P : (j + 1) * P].bitcast(FP8X4),
-                    lhsT_scale=hw_scales[n][:, j * P : (j + 1) * P],
+                    lhsT=hw_codes[pair][:, hw_cols].bitcast(FP8X4),
+                    lhsT_scale=hw_scales[pair][:, hw_cols],
                     rhs=b_codes[:].bitcast(FP8X4),
                     rhs_scale=b_scales[:],
                     start=False,
@@ -488,7 +506,7 @@ def tile_linearmoloralayer_pa_t_kernel(tc, x, gate_logits, W_base, b_base, A, B,
                     transpose_x(unit)
             if n == 1:
                 spread_rest()
-                load_x(10 * UNIT, SLOTS)
+                load_x(9 * UNIT, SLOTS)
             if FIRST_SORTED <= n + 4 < UNITS:
                 sort_x(n + 4)
             if n + 1 < UNITS:

@@ -57,8 +57,7 @@ def tile_linearmoloralayer_pa_t_kernel(tc, x, gate_logits, W_base, b_base, A, B,
         hwq_pool = ctx.enter_context(tc.tile_pool(name="hwq_pool", bufs=LAG))
         stage_pool = ctx.enter_context(tc.tile_pool(name="stage_pool", bufs=6))
         t_psum = ctx.enter_context(tc.psum_pool(name="t_psum", bufs=4))
-        h_psum = ctx.enter_context(tc.psum_pool(name="h_psum", bufs=2))
-        o_psum = ctx.enter_context(tc.psum_pool(name="o_psum", bufs=2))
+        w_psum = ctx.enter_context(tc.psum_pool(name="w_psum", bufs=4))
         ctx.enter_context(tc.manual_schedule())
 
         ident = keep.tile([P, P], F32)
@@ -337,10 +336,8 @@ def tile_linearmoloralayer_pa_t_kernel(tc, x, gate_logits, W_base, b_base, A, B,
         def open_h(n):
             h_banks[n] = []
             for j in range(UNIT):
-                if n == 1:
-                    h_bank = o_psum.tile([P, BANK], F32, name="h_early", tag="o")
-                elif n < UNITS - 1:
-                    h_bank = h_psum.tile([P, BANK], F32, name="h_bank", tag="h")
+                if n < UNITS - 1:
+                    h_bank = w_psum.tile([P, BANK], F32, name="h_bank", tag="w")
                 else:
                     h_bank = t_psum.tile([P, BANK], F32, name="h_last", tag="t")
                 h_banks[n].append(h_bank)
@@ -394,10 +391,7 @@ def tile_linearmoloralayer_pa_t_kernel(tc, x, gate_logits, W_base, b_base, A, B,
 
         def emit_output(n):
             if n < UNITS - 1:
-                if n < UNITS - 2:
-                    bank = o_psum.tile([P, BANK], F32, name="o_bank", tag="o")
-                else:
-                    bank = h_psum.tile([P, BANK], F32, name="o_late", tag="h")
+                bank = w_psum.tile([P, BANK], F32, name="o_bank", tag="w")
                 o_slots[n] = [bank[:, j * O : (j + 1) * O] for j in range(UNIT)]
                 o_pieces[n] = [(0, UNIT, bank[:])]
             else:

from contextlib import ExitStack

import concourse.masks as masks
import concourse.mybir as mybir

F32 = mybir.dt.float32
BF16 = mybir.dt.bfloat16
U32 = mybir.dt.uint32
U8 = mybir.dt.uint8
FP8X4 = mybir.dt.float8_e4m3fn_x4
ALU = mybir.AluOpType
ACT = mybir.ActivationFunctionType
AXIS = mybir.AxisListType

P = 128
PACK = 4
TOKENS = 4096
D = 1024
O = 256
E = 32
RANK = 16
ER = E * RANK
SCALING = 2.0
PASSES = D // (P * PACK)
WORDS = D // 2
BANK = 512
SLOTS = TOKENS // P
UNIT = 2
UNITS = SLOTS // UNIT
O_TILES = O // P
LAG = 3
QUICK = 8
HEAD = 8
GROUP = P // E
FIRST_SORTED = 5

FLOPS = 2 * TOKENS * D * (O + ER) + 2 * TOKENS * ER * O


def tile_linearmoloralayer_pa_t_kernel(tc, x, gate_logits, W_base, b_base, A, B, out):
    nc = tc.nc

    x_view = x.flatten_outer_dims().rearrange("(p s) d -> p s d", s=SLOTS)
    gate_view = gate_logits.flatten_outer_dims().rearrange("(p s) e -> p (s e)", s=SLOTS)
    out_view = out.flatten_outer_dims().rearrange("(p s) o -> p s o", s=SLOTS)
    a_view = A.flatten_outer_dims().rearrange("(q c) d -> q c d", c=PACK)
    w_view = W_base.rearrange("(h m) d -> m h d", m=P)
    b_view = B.rearrange("e (m h) r -> m e (h r)", h=O_TILES)

    with ExitStack() as ctx:
        keep = ctx.enter_context(tc.tile_pool(name="keep", bufs=1))
        sort_pool = ctx.enter_context(tc.tile_pool(name="sort_pool", bufs=4))
        xg_pool = ctx.enter_context(tc.tile_pool(name="xg_pool", bufs=4))
        xq_pool = ctx.enter_context(tc.tile_pool(name="xq_pool", bufs=LAG + 2))
        route_pool = ctx.enter_context(tc.tile_pool(name="route_pool", bufs=4))
        hwg_pool = ctx.enter_context(tc.tile_pool(name="hwg_pool", bufs=2))
        hwq_pool = ctx.enter_context(tc.tile_pool(name="hwq_pool", bufs=LAG))
        stage_pool = ctx.enter_context(tc.tile_pool(name="stage_pool", bufs=6))
        t_psum = ctx.enter_context(tc.psum_pool(name="t_psum", bufs=4))
        w_psum = ctx.enter_context(tc.psum_pool(name="w_psum", bufs=4))
        ctx.enter_context(tc.manual_schedule())

        ident = keep.tile([P, P], F32)
        masks.make_identity(nc, ident[:])

        gate_sb = keep.tile([P, SLOTS * E], BF16)
        a_raw = [keep.tile([P, D], BF16, name="a_raw%d" % c) for c in range(PACK)]
        x_raw = [keep.tile([P, D], BF16, name="x_raw%d" % s) for s in range(SLOTS)]
        w_raw = keep.tile([P, O_TILES * D], BF16)
        b_raw = keep.tile([P, O_TILES * ER], BF16)
        bias_sb = keep.tile([P, O], BF16)

        def load_x(first, last):
            for s in range(first, last):
                nc.sync.dma_start(out=x_raw[s][:], in_=x_view[:, s, :])

        nc.sync.dma_start(out=gate_sb[:, : QUICK * E], in_=gate_view[:, : QUICK * E])
        load_x(0, UNIT)
        for c in range(PACK):
            nc.sync.dma_start(out=a_raw[c][:], in_=a_view[:, c, :])
        load_x(UNIT, 2 * UNIT)
        nc.sync.dma_start(out=gate_sb[:, QUICK * E :], in_=gate_view[:, QUICK * E :])
        load_x(2 * UNIT, 3 * UNIT)
        nc.sync.dma_start(out=w_raw[:].rearrange("m (h d) -> m h d", h=O_TILES), in_=w_view)
        nc.sync.dma_start(out=b_raw[:].rearrange("m (e f) -> m e f", e=E), in_=b_view)
        load_x(3 * UNIT, 9 * UNIT)
        nc.sync.dma_start(out=bias_sb[:], in_=b_base.partition_broadcast(P))

        def transpose_rows(bank, words):
            for g in range(PASSES):
                for u in range(2):
                    cols = slice((g * 2 + u) * P, (g * 2 + u + 1) * P)
                    every_second = slice(g * 2 * P + u, (g + 1) * 2 * P, 2)
                    nc.tensor.transpose(out=bank[:, cols], in_=words[:, every_second], identity=ident[:])

        def transpose_sorted_rows(bank, words):
            for block in range(WORDS // P):
                cols = slice(block * P, (block + 1) * P)
                nc.tensor.transpose(out=bank[:, cols], in_=words[:, cols], identity=ident[:])

        def words_side_by_side(bank):
            return bank[:].rearrange("q (g u m) -> q g m u", g=PASSES, u=2)

        g_max = keep.tile([P, SLOTS], F32)
        g_exp = keep.tile([P, SLOTS * E], F32)
        g_sum = keep.tile([P, SLOTS], F32)
        g_inv = keep.tile([P, SLOTS], F32)
        route_wide = {}
        route_t = {}

        def by_slot(ap):
            return ap.rearrange("p (s e) -> p s e", e=E)

        def softmax_max(first, last):
            cols = slice(first * E, last * E)
            nc.vector.tensor_reduce(
                out=g_max[:, first:last], in_=by_slot(gate_sb[:, cols]), axis=AXIS.X, op=ALU.max
            )

        def softmax_shift(first, last):
            cols = slice(first * E, last * E)
            engine = nc.vector if first == 0 else nc.vector
            engine.tensor_tensor(
                out=by_slot(g_exp[:, cols]),
                in0=by_slot(gate_sb[:, cols]),
                in1=g_max[:, first:last].unsqueeze(2).to_broadcast([P, last - first, E]),
                op=ALU.subtract,
            )

        def softmax_exp(first, last):
            cols = slice(first * E, last * E)
            nc.scalar.activation(out=g_exp[:, cols], in_=g_exp[:, cols], func=ACT.Exp)

        def softmax_sum(first, last):
            cols = slice(first * E, last * E)
            nc.vector.tensor_reduce(
                out=g_sum[:, first:last], in_=by_slot(g_exp[:, cols]), axis=AXIS.X, op=ALU.add
            )
            nc.vector.reciprocal(out=g_inv[:, first:last], in_=g_sum[:, first:last])

        def expand_route(n):
            first = n * UNIT
            wide = route_pool.tile([P, UNIT * P], F32, name="route_wide", tag="route_wide")
            route_wide[n] = wide
            if n == 0:
                shape = [P, UNIT, E, PACK]
                nc.vector.tensor_tensor(
                    out=wide[:].rearrange("p (j e i) -> p j e i", j=UNIT, i=PACK),
                    in0=by_slot(g_exp[:, first * E : (first + UNIT) * E]).unsqueeze(3).to_broadcast(shape),
                    in1=g_inv[:, first : first + UNIT].unsqueeze(2).unsqueeze(3).to_broadcast(shape),
                    op=ALU.mult,
                )
                return
            for slot in range(first, first + UNIT):
                nc.scalar.activation(
                    out=wide[:, (slot - first) * P : (slot - first + 1) * P].rearrange(
                        "p (e i) -> p e i", i=PACK
                    ),
                    in_=g_exp[:, slot * E : (slot + 1) * E].unsqueeze(2).to_broadcast([P, E, PACK]),
                    func=ACT.Copy,
                    scale=g_inv[:, slot : slot + 1],
                )

        def transpose_route(n):
            bank = t_psum.tile([P, UNIT * P], F32, name="route_bank", tag="t")
            for j in range(UNIT):
                cols = slice(j * P, (j + 1) * P)
                nc.tensor.transpose(out=bank[:, cols], in_=route_wide[n][:, cols], identity=ident[:])
            route_t[n] = route_pool.tile([P, UNIT * P], F32, name="route_t", tag="route_t")
            nc.scalar.mul(out=route_t[n][:], in_=bank[:], mul=SCALING)

        def route_columns(n, j):
            slot = n * UNIT + j
            if slot < HEAD:
                return route_t[n][:, j * P : (j + 1) * P]
            group, a = divmod(slot - HEAD, GROUP)
            first = a * REST_COLS + group * P
            return route_rest[:, first : first + P]

        REST = SLOTS - HEAD
        GROUPS = REST // GROUP
        REST_COLS = GROUPS * P
        route_norm = keep.tile([P, REST * E], F32)
        route_turned = keep.tile([P, REST_COLS], F32)
        route_rest = keep.tile([P, GROUP * REST_COLS], F32)

        def normalise_rest():
            nc.vector.tensor_tensor(
                out=route_norm[:].rearrange("p (g e a) -> p g e a", e=E, a=GROUP),
                in0=g_exp[:, HEAD * E :].rearrange("p (g a e) -> p g e a", a=GROUP, e=E),
                in1=g_inv[:, HEAD:]
                .rearrange("p (g a) -> p g a", a=GROUP)
                .unsqueeze(2)
                .to_broadcast([P, GROUPS, E, GROUP]),
                op=ALU.mult,
            )

        def turn_rest():
            for first in range(0, GROUPS, BANK // P):
                count = min(BANK // P, GROUPS - first)
                bank = t_psum.tile([P, BANK], F32, name="rest_bank", tag="t")
                for k in range(count):
                    cols = slice((first + k) * P, (first + k + 1) * P)
                    nc.tensor.transpose(
                        out=bank[:, k * P : (k + 1) * P], in_=route_norm[:, cols], identity=ident[:]
                    )
                nc.scalar.mul(
                    out=route_turned[:, first * P : (first + count) * P],
                    in_=bank[:, : count * P],
                    mul=SCALING,
                )

        def spread_rest():
            for a in range(GROUP):
                for i in range(P // E):
                    nc.sync.dma_start(
                        out=route_rest[i : P : P // E, a * REST_COLS : (a + 1) * REST_COLS],
                        in_=route_turned[a : P : GROUP, :],
                    )

        a_grouped = keep.tile([P, PACK * D], BF16, align_bytes=64)
        a_codes = keep.tile([P, PACK * PASSES * P], U32, align_bytes=64)
        a_scales = keep.tile([P, PACK * PASSES * P], U8, align_bytes=64)
        w_grouped = keep.tile([P, O_TILES * D], BF16, align_bytes=64)
        w_codes = keep.tile([P, PASSES * O], U32, align_bytes=64)
        w_scales = keep.tile([P, PASSES * O], U8, align_bytes=64)
        b_sorted = keep.tile([P, O_TILES * ER], BF16)
        b_grouped = keep.tile([P, O * PACK], BF16, align_bytes=64)
        b_codes = keep.tile([P, O], U32, align_bytes=64)
        b_scales = keep.tile([P, O], U8, align_bytes=64)

        def transpose_a(c):
            bank = t_psum.tile([P, BANK], F32, name="a_bank", tag="t")
            transpose_rows(bank, a_raw[c][:].bitcast(F32))
            grouped_words = a_grouped[:].bitcast(F32).rearrange(
                "q (c g m u) -> q c g m u", c=PACK, g=PASSES, u=2
            )
            nc.scalar.copy(out=grouped_words[:, c], in_=words_side_by_side(bank))

        def quantise_a(c):
            cols = slice(c * PASSES * P, (c + 1) * PASSES * P)
            nc.vector.quantize_mx(
                out=a_codes[:, cols].bitcast(FP8X4),
                scales=a_scales[:, cols],
                in_=a_grouped[:, c * D : (c + 1) * D],
            )

        def transpose_w():
            grouped_words = w_grouped[:].bitcast(F32).rearrange(
                "q (g h m u) -> q g h m u", g=PASSES, h=O_TILES, u=2
            )
            for h in range(O_TILES):
                bank = t_psum.tile([P, BANK], F32, name="w_bank", tag="t")
                transpose_rows(bank, w_raw[:].bitcast(F32)[:, h * WORDS : (h + 1) * WORDS])
                nc.scalar.copy(out=grouped_words[:, :, h], in_=words_side_by_side(bank))

        def quantise_w():
            nc.vector.quantize_mx(
                out=w_codes[:].bitcast(FP8X4), scales=w_scales[:], in_=w_grouped[:]
            )

        def sort_b():
            for h in range(O_TILES):
                nc.scalar.copy(
                    out=b_sorted[:].bitcast(F32)[:, h * ER // 2 : (h + 1) * ER // 2].rearrange(
                        "m (u e v) -> m e v u", u=2, e=E
                    ),
                    in_=b_raw[:].bitcast(F32).rearrange("m (e h v u) -> m h e v u", h=O_TILES, e=E, u=2)[:, h],
                )

        def transpose_b():
            words = b_sorted[:].bitcast(F32).rearrange("m (h u q) -> m h u q", h=O_TILES, u=2)
            bank = t_psum.tile([P, BANK], F32, name="b_bank", tag="t")
            for h in range(O_TILES):
                for u in range(2):
                    cols = slice((h * 2 + u) * P, (h * 2 + u + 1) * P)
                    nc.tensor.transpose(out=bank[:, cols], in_=words[:, h, u, :], identity=ident[:])
            nc.scalar.copy(
                out=b_grouped[:].bitcast(F32).rearrange("q (m h u) -> q m h u", h=O_TILES, u=2),
                in_=bank[:].rearrange("q (h u m) -> q m h u", h=O_TILES, u=2),
            )

        def quantise_b():
            nc.vector.quantize_mx(
                out=b_codes[:].bitcast(FP8X4), scales=b_scales[:], in_=b_grouped[:]
            )

        x_sorted = {}
        x_grouped = {}
        x_codes = {}
        x_scales = {}

        def sort_x(n):
            x_sorted[n] = sort_pool.tile([P, UNIT * D], BF16, name="x_sorted", tag="xsort", align_bytes=64)
            words = x_sorted[n][:].bitcast(F32)
            for j in range(UNIT):
                nc.scalar.copy(
                    out=words[:, j * WORDS : (j + 1) * WORDS].rearrange(
                        "p (g u q) -> p g u q", g=PASSES, u=2
                    ),
                    in_=x_raw[n * UNIT + j][:].bitcast(F32).rearrange(
                        "p (g q u) -> p g u q", g=PASSES, u=2
                    ),
                )

        def transpose_x(n):
            x_grouped[n] = xg_pool.tile([P, UNIT * D], BF16, name="x_grouped", tag="xg", align_bytes=64)
            grouped_words = x_grouped[n][:].bitcast(F32).rearrange(
                "q (j g w u) -> q j g w u", j=UNIT, g=PASSES, u=2
            )
            for j in range(UNIT):
                bank = t_psum.tile([P, BANK], F32, name="x_bank", tag="t")
                if n < FIRST_SORTED:
                    transpose_rows(bank, x_raw[n * UNIT + j][:].bitcast(F32))
                else:
                    words = x_sorted[n][:].bitcast(F32)
                    transpose_sorted_rows(bank, words[:, j * WORDS : (j + 1) * WORDS])
                copy = nc.vector.tensor_copy if (n, j) == (0, 1) else nc.scalar.copy
                copy(out=grouped_words[:, j], in_=words_side_by_side(bank))

        def quantise_x(n):
            width = UNIT * PASSES * P
            x_codes[n] = xq_pool.tile([P, width], U32, name="x_codes", tag="xc", align_bytes=64)
            x_scales[n] = xq_pool.tile([P, width], U8, name="x_scales", tag="xs", align_bytes=64)
            nc.vector.quantize_mx(
                out=x_codes[n][:].bitcast(FP8X4), scales=x_scales[n][:], in_=x_grouped[n][:]
            )

        hw_grouped = {}
        hw_codes = {}
        hw_scales = {}
        h_banks = {}
        o_slots = {}
        o_pieces = {}

        def open_h(n):
            h_banks[n] = []
            for j in range(UNIT):
                if n < UNITS - 1:
                    h_bank = w_psum.tile([P, BANK], F32, name="h_bank", tag="w")
                else:
                    h_bank = t_psum.tile([P, BANK], F32, name="h_last", tag="t")
                h_banks[n].append(h_bank)

        def project(n, chunks):
            for j in range(UNIT):
                h_bank = h_banks[n][j]
                for c in chunks:
                    for g in range(PASSES):
                        a_cols = slice((c * PASSES + g) * P, (c * PASSES + g + 1) * P)
                        x_cols = slice((j * PASSES + g) * P, (j * PASSES + g + 1) * P)
                        nc.tensor.matmul_mx(
                            out=h_bank[:, c * P : (c + 1) * P],
                            lhsT=a_codes[:, a_cols].bitcast(FP8X4),
                            lhsT_scale=a_scales[:, a_cols],
                            rhs=x_codes[n][:, x_cols].bitcast(FP8X4),
                            rhs_scale=x_scales[n][:, x_cols],
                            start=(g == 0),
                            stop=(g == PASSES - 1),
                        )

        def gate_h(n):
            pair, place = divmod(n + 1, 2)
            if pair not in hw_grouped:
                hw_grouped[pair] = hwg_pool.tile(
                    [P, 2 * UNIT * ER], BF16, name="hw_grouped", tag="hwg", align_bytes=64
                )
            for j in range(UNIT):
                first = (place * UNIT + j) * ER
                nc.vector.tensor_tensor(
                    out=hw_grouped[pair][:, first : first + ER].rearrange("q (w c) -> q w c", c=PACK),
                    in0=h_banks[n][j][:].rearrange("q (c w) -> q w c", c=PACK),
                    in1=route_columns(n, j).unsqueeze(2).to_broadcast([P, P, PACK]),
                    op=ALU.mult,
                )

        def quantise_hw(n):
            if n % 2 == 1 and n < UNITS - 1:
                return
            pair = (n + 1) // 2
            first = 1 if n == 0 else 0
            last = 1 if n == UNITS - 1 else 2
            hw_codes[pair] = hwq_pool.tile([P, 2 * UNIT * P], U32, name="hw_codes", tag="hc", align_bytes=64)
            hw_scales[pair] = hwq_pool.tile([P, 2 * UNIT * P], U8, name="hw_scales", tag="hs", align_bytes=64)
            cols = slice(first * UNIT * P, last * UNIT * P)
            nc.vector.quantize_mx(
                out=hw_codes[pair][:, cols].bitcast(FP8X4),
                scales=hw_scales[pair][:, cols],
                in_=hw_grouped[pair][:, first * UNIT * ER : last * UNIT * ER],
            )

        def emit_output(n):
            if n < UNITS - 1:
                bank = w_psum.tile([P, BANK], F32, name="o_bank", tag="w")
                o_slots[n] = [bank[:, j * O : (j + 1) * O] for j in range(UNIT)]
                o_pieces[n] = [(0, UNIT, bank[:])]
            else:
                o_slots[n] = []
                o_pieces[n] = []
                for j in range(UNIT):
                    bank = t_psum.tile([P, BANK], F32, name="o_last", tag="t")
                    o_slots[n].append(bank[:, :O])
                    o_pieces[n].append((j, 1, bank[:, :O]))
            for j in range(UNIT):
                for g in range(PASSES):
                    x_cols = slice((j * PASSES + g) * P, (j * PASSES + g + 1) * P)
                    nc.tensor.matmul_mx(
                        out=o_slots[n][j],
                        lhsT=x_codes[n][:, x_cols].bitcast(FP8X4),
                        lhsT_scale=x_scales[n][:, x_cols],
                        rhs=w_codes[:, g * O : (g + 1) * O].bitcast(FP8X4),
                        rhs_scale=w_scales[:, g * O : (g + 1) * O],
                        start=(g == 0),
                        stop=False,
                    )
                pair, place = divmod(n + 1, 2)
                hw_cols = slice((place * UNIT + j) * P, (place * UNIT + j + 1) * P)
                nc.tensor.matmul_mx(
                    out=o_slots[n][j],
                    lhsT=hw_codes[pair][:, hw_cols].bitcast(FP8X4),
                    lhsT_scale=hw_scales[pair][:, hw_cols],
                    rhs=b_codes[:].bitcast(FP8X4),
                    rhs_scale=b_scales[:],
                    start=False,
                    stop=True,
                )

        def add_bias_and_store(n):
            o_stage = stage_pool.tile([P, UNIT * O], F32, name="o_stage", tag="os")
            for first, count, piece in o_pieces[n]:
                staged = o_stage[:, first * O : (first + count) * O].rearrange("p (j o) -> p j o", o=O)
                nc.vector.tensor_tensor(
                    out=staged,
                    in0=piece.rearrange("p (j o) -> p j o", o=O),
                    in1=bias_sb[:].unsqueeze(1).to_broadcast([P, count, O]),
                    op=ALU.add,
                )
                slot = n * UNIT + first
                nc.sync.dma_start(out=out_view[:, slot : slot + count, :], in_=staged)

        warm = keep.tile([P, 1], F32)
        nc.vector.memset(warm[:], 0.0)
        nc.scalar.activation(out=warm[:], in_=warm[:], func=ACT.Exp)

        softmax_max(0, QUICK)
        softmax_shift(0, QUICK)
        softmax_exp(0, QUICK)
        softmax_sum(0, QUICK)
        expand_route(0)
        transpose_x(0)
        quantise_x(0)
        transpose_a(0)
        transpose_a(1)
        transpose_route(0)
        transpose_a(2)
        transpose_a(3)
        for c in range(PACK):
            quantise_a(c)
        softmax_max(QUICK, SLOTS)
        softmax_shift(QUICK, SLOTS)
        expand_route(1)
        expand_route(2)
        expand_route(3)
        open_h(0)
        project(0, (0,))
        project(0, (1,))
        transpose_x(1)
        transpose_route(1)
        project(0, (2,))
        project(0, (3,))
        softmax_exp(QUICK, SLOTS)

        for n in range(UNITS + LAG):
            if 0 < n < UNITS:
                open_h(n)
                if n == 1:
                    project(n, (0, 1))
                    transpose_w()
                    project(n, (2, 3))
                elif n == 2:
                    project(n, (0, 1))
                    transpose_b()
                    project(n, (2, 3))
                else:
                    project(n, range(PACK))
            if n >= LAG:
                emit_output(n - LAG)
            if n == 0:
                transpose_x(2)
                transpose_route(2)
            if n == 1:
                transpose_x(3)
                transpose_route(3)
                turn_rest()
            if n == 2:
                transpose_x(4)
                transpose_x(5)
            if n >= 4 and n % 2 == 0:
                for unit in range(n + 2, min(n + 4, UNITS)):
                    transpose_x(unit)
            if n == 1:
                spread_rest()
                load_x(9 * UNIT, SLOTS)
            if FIRST_SORTED <= n + 4 < UNITS:
                sort_x(n + 4)
            if n + 1 < UNITS:
                quantise_x(n + 1)
            if n < UNITS:
                gate_h(n)
            if n >= LAG:
                add_bias_and_store(n - LAG)
            if n < UNITS:
                quantise_hw(n)
            if n == 0:
                softmax_sum(QUICK, SLOTS)
            if n == 0:
                normalise_rest()
            if n == 0:
                sort_b()
            if n == 2:
                quantise_w()
            if n == 2:
                quantise_b()
